import numpy as np
import ml_dtypes


def mxq(x, axis, fmt="e4m3"):
    dtype, down = {"e4m3": (ml_dtypes.float8_e4m3fn, 7), "e5m2": (ml_dtypes.float8_e5m2, 14)}[fmt]
    v = np.moveaxis(np.asarray(x, np.float32).astype(ml_dtypes.bfloat16).astype(np.float64), axis, -1)
    blocks = v.reshape(v.shape[:-1] + (-1, 32))
    amax = np.abs(blocks).max(-1, keepdims=True)
    byte = np.maximum(np.where(amax > 0, np.frexp(amax)[1] - 1 + 127, 0) - down, 1)
    scale = np.exp2(byte - 127.0)
    codes = (blocks / scale).astype(np.float32).astype(dtype).astype(np.float64)
    return np.moveaxis((codes * scale).reshape(v.shape), -1, axis)


WIDE = False


def mx_kscale(k):
    if not WIDE:
        return np.ones(k)
    levels = np.array([10, -10, 5, -5, 0])
    a = np.random.permutation(np.resize(levels, k // 512 * 4)).reshape(k // 512, 4)
    idx = np.arange(k)
    return np.exp2(a[idx // 512, idx % 128 // 32])


BF16 = ml_dtypes.bfloat16


def bf(x):
    return np.asarray(x, np.float32).astype(BF16)


def f64(x):
    return np.asarray(x).astype(np.float64)


B, D, U = 256, 1024, 128


def sigmoid(v):
    return 1.0 / (1.0 + np.exp(-v))


def setup_inputs():
    s = mx_kscale(D)
    inp = {"pre_layer": bf(np.random.standard_normal((2, B, U))), "x": bf(np.random.standard_normal((B, D)) * s)}
    for n in ("W_i", "W_f", "W_o", "W_c"):
        inp[n] = bf(np.random.standard_normal((D, U)) / np.sqrt(D) / s[:, None])
    for n in ("U_i", "U_f", "U_o", "U_c"):
        inp[n] = bf(np.random.standard_normal((U, U)) / np.sqrt(U))
    return inp


def reference(pre_layer, x, W_i, W_f, W_o, W_c, U_i, U_f, U_o, U_c):
    pre = f64(pre_layer)
    pre_h, pre_c = pre[0], pre[1]
    W = np.concatenate([f64(W_i), f64(W_f), f64(W_o), f64(W_c)], axis=1)
    Uw = np.concatenate([f64(U_i), f64(U_f), f64(U_o), f64(U_c)], axis=1)
    gates = (mxq(f64(x), 1, "e4m3") @ mxq(W, 0, "e4m3")) + pre_h @ Uw
    zi, zf, zo, zc = np.split(gates, 4, axis=1)
    i_t = sigmoid(zi)
    f_t = sigmoid(zf)
    o_t = sigmoid(zo)
    n_c_t = np.tanh(zc)
    c = f_t * pre_c + i_t * n_c_t
    h = o_t * np.tanh(c)
    return np.stack([h, c])

@@ -1,0 +1,165 @@
+from contextlib import ExitStack
+
+import concourse.mybir as mybir
+from concourse.masks import make_identity
+
+F32 = mybir.dt.float32
+BF16 = mybir.dt.bfloat16
+U32 = mybir.dt.uint32
+U8 = mybir.dt.uint8
+FP8X4 = mybir.dt.float8_e4m3fn_x4
+ACT = mybir.ActivationFunctionType
+
+P = 128
+BATCH = 256
+D_IN = 1024
+UNITS = 128
+GATES = 4
+PACK = 4
+PAIRS = PACK // 2
+K_PASS = P * PACK
+PASSES = D_IN // K_PASS
+B_TILES = BATCH // P
+
+VECTOR_COLS = 96
+RUN = 4
+
+FLOPS = 2 * BATCH * (D_IN + UNITS) * GATES * UNITS
+
+
+def tile_lstm_s_kernel(tc, pre_layer, x, W_i, W_f, W_o, W_c, U_i, U_f, U_o, U_c, out):
+    nc = tc.nc
+    w_dram = (W_i, W_f, W_c, W_o)
+    u_dram = (U_i, U_f, U_c, U_o)
+    gate_func = (ACT.Sigmoid, ACT.Sigmoid, ACT.Tanh, ACT.Sigmoid)
+
+    with ExitStack() as stack:
+        keep = stack.enter_context(tc.tile_pool(name="keep", bufs=1))
+        psum_h = stack.enter_context(tc.psum_pool(name="psum_h", bufs=1))
+        psum_x = stack.enter_context(tc.psum_pool(name="psum_x", bufs=B_TILES))
+        psum_rec = stack.enter_context(tc.psum_pool(name="psum_rec", bufs=B_TILES))
+        psum_gate = stack.enter_context(tc.psum_pool(name="psum_gate", bufs=3))
+
+        x_rows = x.rearrange("(p t) k -> t p k", t=B_TILES)
+        x_sb = []
+        for t in range(B_TILES):
+            x_t = keep.tile([P, D_IN], BF16, name="x_sb%d" % t)
+            nc.sync.dma_start(out=x_t[:], in_=x_rows[t])
+            x_sb.append(x_t)
+
+        pre_sb = keep.tile([P, 2, B_TILES, UNITS], BF16)
+        nc.scalar.dma_start(out=pre_sb[:], in_=pre_layer.rearrange("s (p t) u -> p s t u", t=B_TILES))
+        pre_h = pre_sb[:, 0]
+        pre_c = pre_sb[:, 1]
+
+        u_sb = keep.tile([P, GATES, UNITS], BF16)
+        for g in range(GATES):
+            nc.scalar.dma_start(out=u_sb[:, g, :], in_=u_dram[g])
+
+        w_raw = []
+        for g in range(GATES):
+            w_g = keep.tile([P, PASSES, PACK, UNITS], BF16, name="w_raw%d" % g)
+            nc.sync.dma_start(out=w_g[:], in_=w_dram[g].rearrange("(c p j) w -> p c j w", c=PASSES, j=PACK))
+            w_raw.append(w_g)
+
+        ident_f32 = keep.tile([P, P], F32)
+        make_identity(nc, ident_f32[:])
+        ident_bf16 = keep.tile([P, P], BF16)
+        make_identity(nc, ident_bf16[:])
+
+        table_in = keep.tile([P, 1], F32)
+        table_out = keep.tile([P, 1], F32)
+        nc.vector.memset(table_in[:], 0.0)
+        nc.scalar.activation(out=table_out[:], in_=table_in[:], func=ACT.Sigmoid)
+
+        hT_ps = psum_h.tile([P, B_TILES, P], BF16)
+        for t in range(B_TILES):
+            nc.tensor.transpose(hT_ps[:, t, :], pre_h[:, t, :], ident_bf16[:])
+        hT_sb = keep.tile([P, B_TILES, P], BF16)
+        nc.scalar.copy(out=hT_sb[:], in_=hT_ps[:])
+
+        rec_sb = keep.tile([P, GATES, B_TILES, UNITS], F32)
+        for t in range(B_TILES):
+            rec_ps = psum_rec.tile([P, GATES, UNITS], F32)
+            nc.tensor.matmul(
+                out=rec_ps[:].rearrange("p g u -> p (g u)"),
+                lhsT=hT_sb[:, t, :],
+                rhs=u_sb[:].rearrange("p g u -> p (g u)"),
+                start=True,
+                stop=True,
+            )
+            nc.scalar.copy(out=rec_sb[:, :, t, :], in_=rec_ps[:])
+
+        x_codes = []
+        x_scales = []
+        for t in range(B_TILES):
+            x_words = x_sb[t][:].bitcast(F32).rearrange("p (c q u) -> p c u q", c=PASSES, u=PAIRS)
+            xT_ps = psum_x.tile([P, PASSES, PAIRS, P], F32)
+            for c in range(PASSES):
+                for u in range(PAIRS):
+                    nc.tensor.transpose(xT_ps[:, c, u, :], x_words[:, c, u, :], ident_f32[:])
+            x_grouped = keep.tile([P, PASSES * P * PACK], BF16, align_bytes=64, name="x_grouped%d" % t)
+            nc.scalar.copy(
+                out=x_grouped[:].bitcast(F32).rearrange("p (c b u) -> p c b u", c=PASSES, u=PAIRS),
+                in_=xT_ps[:].rearrange("p c u b -> p c b u"),
+            )
+            codes = keep.tile([P, PASSES * P], U32, align_bytes=64, name="x_codes%d" % t)
+            scales = keep.tile([P, PASSES * P], U8, align_bytes=64, name="x_scales%d" % t)
+            nc.vector.quantize_mx(out=codes[:].bitcast(FP8X4), scales=scales[:], in_=x_grouped[:])
+            x_codes.append(codes)
+            x_scales.append(scales)
+
+        gate = []
+        for g in range(GATES):
+            w_grouped = keep.tile([P, PASSES, UNITS, PACK], BF16, align_bytes=64, name="w_grouped%d" % g)
+            for c in range(PASSES):
+                nc.vector.tensor_copy(
+                    out=w_grouped[:, c, :VECTOR_COLS, :].rearrange("p (a i) j -> p a j i", i=RUN),
+                    in_=w_raw[g][:, c, :, :VECTOR_COLS].rearrange("p j (a i) -> p a j i", i=RUN),
+                )
+                nc.scalar.copy(
+                    out=w_grouped[:, c, VECTOR_COLS:, :].rearrange("p (a i) j -> p a j i", i=RUN),
+                    in_=w_raw[g][:, c, :, VECTOR_COLS:].rearrange("p j (a i) -> p a j i", i=RUN),
+                )
+            w_codes = keep.tile([P, PASSES * UNITS], U32, align_bytes=64, name="w_codes%d" % g)
+            w_scales = keep.tile([P, PASSES * UNITS], U8, align_bytes=64, name="w_scales%d" % g)
+            nc.vector.quantize_mx(
+                out=w_codes[:].bitcast(FP8X4),
+                scales=w_scales[:],
+                in_=w_grouped[:].rearrange("p c w j -> p (c w j)"),
+            )
+
+            acc = psum_gate.tile([P, B_TILES, UNITS], F32)
+            for t in range(B_TILES):
+                for c in range(PASSES):
+                    cols = slice(c * P, (c + 1) * P)
+                    nc.tensor.matmul_mx(
+                        out=acc[:, t, :],
+                        lhsT=x_codes[t][:, cols].bitcast(FP8X4),
+                        lhsT_scale=x_scales[t][:, cols],
+                        rhs=w_codes[:, cols].bitcast(FP8X4),
+                        rhs_scale=w_scales[:, cols],
+                        start=(c == 0),
+                        stop=(c == PASSES - 1),
+                    )
+
+            z = keep.tile([P, B_TILES, UNITS], F32, name="z%d" % g)
+            nc.vector.tensor_add(out=z[:], in0=acc[:], in1=rec_sb[:, g])
+            activated = keep.tile([P, B_TILES, UNITS], F32, name="gate%d" % g)
+            nc.scalar.activation(out=activated[:], in_=z[:], func=gate_func[g])
+            gate.append(activated)
+        i_t, f_t, n_t, o_t = gate
+
+        kept = keep.tile([P, B_TILES, UNITS], F32)
+        nc.vector.tensor_mul(out=kept[:], in0=f_t[:], in1=pre_c)
+        fresh = keep.tile([P, B_TILES, UNITS], F32)
+        nc.vector.tensor_mul(out=fresh[:], in0=i_t[:], in1=n_t[:])
+        cell = keep.tile([P, B_TILES, UNITS], F32)
+        nc.vector.tensor_add(out=cell[:], in0=kept[:], in1=fresh[:])
+        nc.sync.dma_start(out=out[1].rearrange("(p t) u -> p t u", t=B_TILES), in_=cell[:])
+
+        cell_tanh = keep.tile([P, B_TILES, UNITS], F32)
+        nc.scalar.activation(out=cell_tanh[:], in_=cell[:], func=ACT.Tanh)
+        hidden = keep.tile([P, B_TILES, UNITS], F32)
+        nc.vector.tensor_mul(out=hidden[:], in0=o_t[:], in1=cell_tanh[:])
+        nc.sync.dma_start(out=out[0].rearrange("(p t) u -> p t u", t=B_TILES), in_=hidden[:])

@@ -14,12 +14,15 @@ P = 128
 BATCH = 256
 D_IN = 1024
 UNITS = 128
-GATES = 4
 PACK = 4
 PAIRS = PACK // 2
 K_PASS = P * PACK
 PASSES = D_IN // K_PASS
 B_TILES = BATCH // P
+PSUM_BANKS = 8
+
+GATE_I, GATE_F, GATE_N, GATE_O = range(4)
+GATES = 4
 
 VECTOR_COLS = 96
 RUN = 4
@@ -32,35 +35,34 @@ def tile_lstm_s_kernel(tc, pre_layer, x, W_i, W_f, W_o, W_c, U_i, U_f, U_o, U_c,
     w_dram = (W_i, W_f, W_c, W_o)
     u_dram = (U_i, U_f, U_c, U_o)
     gate_func = (ACT.Sigmoid, ACT.Sigmoid, ACT.Tanh, ACT.Sigmoid)
+    tiles = range(B_TILES)
 
     with ExitStack() as stack:
         keep = stack.enter_context(tc.tile_pool(name="keep", bufs=1))
-        psum_h = stack.enter_context(tc.psum_pool(name="psum_h", bufs=1))
-        psum_x = stack.enter_context(tc.psum_pool(name="psum_x", bufs=B_TILES))
-        psum_rec = stack.enter_context(tc.psum_pool(name="psum_rec", bufs=B_TILES))
-        psum_gate = stack.enter_context(tc.psum_pool(name="psum_gate", bufs=3))
+        psum = stack.enter_context(tc.psum_pool(name="psum", bufs=PSUM_BANKS))
+        stack.enter_context(tc.manual_schedule())
+
+        def unit_tile(name):
+            return keep.tile([P, UNITS], F32, name=name)
 
         x_rows = x.rearrange("(p t) k -> t p k", t=B_TILES)
-        x_sb = []
-        for t in range(B_TILES):
-            x_t = keep.tile([P, D_IN], BF16, name="x_sb%d" % t)
-            nc.sync.dma_start(out=x_t[:], in_=x_rows[t])
-            x_sb.append(x_t)
-
+        x_sb = [keep.tile([P, D_IN], BF16, name="x_sb%d" % t) for t in tiles]
+        w_raw = [keep.tile([P, PASSES, PACK, UNITS], BF16, name="w_raw%d" % g) for g in range(GATES)]
         pre_sb = keep.tile([P, 2, B_TILES, UNITS], BF16)
-        nc.scalar.dma_start(out=pre_sb[:], in_=pre_layer.rearrange("s (p t) u -> p s t u", t=B_TILES))
-        pre_h = pre_sb[:, 0]
-        pre_c = pre_sb[:, 1]
-
         u_sb = keep.tile([P, GATES, UNITS], BF16)
-        for g in range(GATES):
-            nc.scalar.dma_start(out=u_sb[:, g, :], in_=u_dram[g])
 
-        w_raw = []
+        def load_w(g):
+            nc.sync.dma_start(out=w_raw[g][:], in_=w_dram[g].rearrange("(c p j) w -> p c j w", c=PASSES, j=PACK))
+
+        for t in tiles:
+            nc.sync.dma_start(out=x_sb[t][:], in_=x_rows[t])
+        load_w(GATE_I)
+        load_w(GATE_F)
+        nc.sync.dma_start(out=pre_sb[:], in_=pre_layer.rearrange("s (p t) u -> p s t u", t=B_TILES))
         for g in range(GATES):
-            w_g = keep.tile([P, PASSES, PACK, UNITS], BF16, name="w_raw%d" % g)
-            nc.sync.dma_start(out=w_g[:], in_=w_dram[g].rearrange("(c p j) w -> p c j w", c=PASSES, j=PACK))
-            w_raw.append(w_g)
+            nc.sync.dma_start(out=u_sb[:, g, :], in_=u_dram[g])
+        load_w(GATE_N)
+        load_w(GATE_O)
 
         ident_f32 = keep.tile([P, P], F32)
         make_identity(nc, ident_f32[:])
@@ -72,94 +74,120 @@ def tile_lstm_s_kernel(tc, pre_layer, x, W_i, W_f, W_o, W_c, U_i, U_f, U_o, U_c,
         nc.vector.memset(table_in[:], 0.0)
         nc.scalar.activation(out=table_out[:], in_=table_in[:], func=ACT.Sigmoid)
 
-        hT_ps = psum_h.tile([P, B_TILES, P], BF16)
-        for t in range(B_TILES):
-            nc.tensor.transpose(hT_ps[:, t, :], pre_h[:, t, :], ident_bf16[:])
+        xT_ps = [psum.tile([P, PASSES, PAIRS, P], F32, tag="bank", name="xT_ps%d" % t) for t in tiles]
+        x_grouped = [keep.tile([P, PASSES * P * PACK], BF16, align_bytes=64, name="x_grouped%d" % t) for t in tiles]
+        x_codes = [keep.tile([P, PASSES * P], U32, align_bytes=64, name="x_codes%d" % t) for t in tiles]
+        x_scales = [keep.tile([P, PASSES * P], U8, align_bytes=64, name="x_scales%d" % t) for t in tiles]
+
+        def transpose_x(t):
+            x_words = x_sb[t][:].bitcast(F32).rearrange("p (c q u) -> p c u q", c=PASSES, u=PAIRS)
+            for c in range(PASSES):
+                for u in range(PAIRS):
+                    nc.tensor.transpose(xT_ps[t][:, c, u, :], x_words[:, c, u, :], ident_f32[:])
+
+        def regroup_x(t):
+            nc.scalar.copy(
+                out=x_grouped[t][:].bitcast(F32).rearrange("p (c b u) -> p c b u", c=PASSES, u=PAIRS),
+                in_=xT_ps[t][:].rearrange("p c u b -> p c b u"),
+            )
+
+        def quantise_x(t):
+            nc.vector.quantize_mx(out=x_codes[t][:].bitcast(FP8X4), scales=x_scales[t][:], in_=x_grouped[t][:])
+
+        w_grouped = [
+            keep.tile([P, PASSES, UNITS, PACK], BF16, align_bytes=64, name="w_grouped%d" % g) for g in range(GATES)
+        ]
+        w_codes = [keep.tile([P, PASSES * UNITS], U32, align_bytes=64, name="w_codes%d" % g) for g in range(GATES)]
+        w_scales = [keep.tile([P, PASSES * UNITS], U8, align_bytes=64, name="w_scales%d" % g) for g in range(GATES)]
+
+        def regroup_w(g):
+            for c in range(PASSES):
+                nc.vector.tensor_copy(
+                    out=w_grouped[g][:, c, :VECTOR_COLS, :].rearrange("p (a i) j -> p a j i", i=RUN),
+                    in_=w_raw[g][:, c, :, :VECTOR_COLS].rearrange("p j (a i) -> p a j i", i=RUN),
+                )
+                nc.scalar.copy(
+                    out=w_grouped[g][:, c, VECTOR_COLS:, :].rearrange("p (a i) j -> p a j i", i=RUN),
+                    in_=w_raw[g][:, c, :, VECTOR_COLS:].rearrange("p j (a i) -> p a j i", i=RUN),
+                )
+
+        def quantise_w(g):
+            nc.vector.quantize_mx(
+                out=w_codes[g][:].bitcast(FP8X4),
+                scales=w_scales[g][:],
+                in_=w_grouped[g][:].rearrange("p c w j -> p (c w j)"),
+            )
+
+        for t in tiles:
+            transpose_x(t)
+        for t, g in zip(tiles, (GATE_I, GATE_F)):
+            regroup_w(g)
+            regroup_x(t)
+            quantise_w(g)
+            quantise_x(t)
+
+        hT_ps = psum.tile([P, B_TILES, P], BF16, tag="bank")
+        for t in tiles:
+            nc.tensor.transpose(hT_ps[:, t, :], pre_sb[:, 0, t, :], ident_bf16[:])
         hT_sb = keep.tile([P, B_TILES, P], BF16)
         nc.scalar.copy(out=hT_sb[:], in_=hT_ps[:])
-
-        rec_sb = keep.tile([P, GATES, B_TILES, UNITS], F32)
-        for t in range(B_TILES):
-            rec_ps = psum_rec.tile([P, GATES, UNITS], F32)
+        rec_ps = [psum.tile([P, GATES * UNITS], F32, tag="bank", name="rec_ps%d" % t) for t in tiles]
+        for t in tiles:
             nc.tensor.matmul(
-                out=rec_ps[:].rearrange("p g u -> p (g u)"),
+                out=rec_ps[t][:],
                 lhsT=hT_sb[:, t, :],
                 rhs=u_sb[:].rearrange("p g u -> p (g u)"),
                 start=True,
                 stop=True,
             )
-            nc.scalar.copy(out=rec_sb[:, :, t, :], in_=rec_ps[:])
 
-        x_codes = []
-        x_scales = []
-        for t in range(B_TILES):
-            x_words = x_sb[t][:].bitcast(F32).rearrange("p (c q u) -> p c u q", c=PASSES, u=PAIRS)
-            xT_ps = psum_x.tile([P, PASSES, PAIRS, P], F32)
-            for c in range(PASSES):
-                for u in range(PAIRS):
-                    nc.tensor.transpose(xT_ps[:, c, u, :], x_words[:, c, u, :], ident_f32[:])
-            x_grouped = keep.tile([P, PASSES * P * PACK], BF16, align_bytes=64, name="x_grouped%d" % t)
-            nc.scalar.copy(
-                out=x_grouped[:].bitcast(F32).rearrange("p (c b u) -> p c b u", c=PASSES, u=PAIRS),
-                in_=xT_ps[:].rearrange("p c u b -> p c b u"),
-            )
-            codes = keep.tile([P, PASSES * P], U32, align_bytes=64, name="x_codes%d" % t)
-            scales = keep.tile([P, PASSES * P], U8, align_bytes=64, name="x_scales%d" % t)
-            nc.vector.quantize_mx(out=codes[:].bitcast(FP8X4), scales=scales[:], in_=x_grouped[:])
-            x_codes.append(codes)
-            x_scales.append(scales)
+        for g in (GATE_N, GATE_O):
+            regroup_w(g)
+        for g in (GATE_N, GATE_O):
+            quantise_w(g)
 
-        gate = []
-        for g in range(GATES):
-            w_grouped = keep.tile([P, PASSES, UNITS, PACK], BF16, align_bytes=64, name="w_grouped%d" % g)
-            for c in range(PASSES):
-                nc.vector.tensor_copy(
-                    out=w_grouped[:, c, :VECTOR_COLS, :].rearrange("p (a i) j -> p a j i", i=RUN),
-                    in_=w_raw[g][:, c, :, :VECTOR_COLS].rearrange("p j (a i) -> p a j i", i=RUN),
-                )
-                nc.scalar.copy(
-                    out=w_grouped[:, c, VECTOR_COLS:, :].rearrange("p (a i) j -> p a j i", i=RUN),
-                    in_=w_raw[g][:, c, :, VECTOR_COLS:].rearrange("p j (a i) -> p a j i", i=RUN),
-                )
-            w_codes = keep.tile([P, PASSES * UNITS], U32, align_bytes=64, name="w_codes%d" % g)
-            w_scales = keep.tile([P, PASSES * UNITS], U8, align_bytes=64, name="w_scales%d" % g)
-            nc.vector.quantize_mx(
-                out=w_codes[:].bitcast(FP8X4),
-                scales=w_scales[:],
-                in_=w_grouped[:].rearrange("p c w j -> p (c w j)"),
-            )
+        rec_sb = [keep.tile([P, GATES, UNITS], F32, name="rec_sb%d" % t) for t in tiles]
+        for t in tiles:
+            nc.scalar.copy(out=rec_sb[t][:].rearrange("p g u -> p (g u)"), in_=rec_ps[t][:])
 
-            acc = psum_gate.tile([P, B_TILES, UNITS], F32)
-            for t in range(B_TILES):
+        gate = [[unit_tile("gate%d_%d" % (g, t)) for t in tiles] for g in range(GATES)]
+
+        def compute_gate(g):
+            for t in tiles:
+                acc = psum.tile([P, UNITS], F32, tag="bank", name="acc%d_%d" % (g, t))
                 for c in range(PASSES):
                     cols = slice(c * P, (c + 1) * P)
                     nc.tensor.matmul_mx(
-                        out=acc[:, t, :],
+                        out=acc[:],
                         lhsT=x_codes[t][:, cols].bitcast(FP8X4),
                         lhsT_scale=x_scales[t][:, cols],
-                        rhs=w_codes[:, cols].bitcast(FP8X4),
-                        rhs_scale=w_scales[:, cols],
+                        rhs=w_codes[g][:, cols].bitcast(FP8X4),
+                        rhs_scale=w_scales[g][:, cols],
                         start=(c == 0),
                         stop=(c == PASSES - 1),
                     )
+                z = unit_tile("z%d_%d" % (g, t))
+                nc.vector.tensor_add(out=z[:], in0=acc[:], in1=rec_sb[t][:, g, :])
+                nc.scalar.activation(out=gate[g][t][:], in_=z[:], func=gate_func[g])
 
-            z = keep.tile([P, B_TILES, UNITS], F32, name="z%d" % g)
-            nc.vector.tensor_add(out=z[:], in0=acc[:], in1=rec_sb[:, g])
-            activated = keep.tile([P, B_TILES, UNITS], F32, name="gate%d" % g)
-            nc.scalar.activation(out=activated[:], in_=z[:], func=gate_func[g])
-            gate.append(activated)
-        i_t, f_t, n_t, o_t = gate
+        for g in (GATE_I, GATE_F, GATE_N):
+            compute_gate(g)
 
-        kept = keep.tile([P, B_TILES, UNITS], F32)
-        nc.vector.tensor_mul(out=kept[:], in0=f_t[:], in1=pre_c)
-        fresh = keep.tile([P, B_TILES, UNITS], F32)
-        nc.vector.tensor_mul(out=fresh[:], in0=i_t[:], in1=n_t[:])
-        cell = keep.tile([P, B_TILES, UNITS], F32)
-        nc.vector.tensor_add(out=cell[:], in0=kept[:], in1=fresh[:])
-        nc.sync.dma_start(out=out[1].rearrange("(p t) u -> p t u", t=B_TILES), in_=cell[:])
-
-        cell_tanh = keep.tile([P, B_TILES, UNITS], F32)
-        nc.scalar.activation(out=cell_tanh[:], in_=cell[:], func=ACT.Tanh)
-        hidden = keep.tile([P, B_TILES, UNITS], F32)
-        nc.vector.tensor_mul(out=hidden[:], in0=o_t[:], in1=cell_tanh[:])
-        nc.sync.dma_start(out=out[0].rearrange("(p t) u -> p t u", t=B_TILES), in_=hidden[:])
+        out_rows = out.rearrange("s (p t) u -> s t p u", t=B_TILES)
+        kept = [unit_tile("kept%d" % t) for t in tiles]
+        fresh = [unit_tile("fresh%d" % t) for t in tiles]
+        cell = [unit_tile("cell%d" % t) for t in tiles]
+        cell_tanh = [unit_tile("cell_tanh%d" % t) for t in tiles]
+        hidden = [unit_tile("hidden%d" % t) for t in tiles]
+        for t in tiles:
+            nc.vector.tensor_mul(out=kept[t][:], in0=gate[GATE_F][t][:], in1=pre_sb[:, 1, t, :])
+        for t in tiles:
+            nc.vector.tensor_mul(out=fresh[t][:], in0=gate[GATE_I][t][:], in1=gate[GATE_N][t][:])
+        compute_gate(GATE_O)
+        for t in tiles:
+            nc.vector.tensor_add(out=cell[t][:], in0=kept[t][:], in1=fresh[t][:])
+            nc.scalar.activation(out=cell_tanh[t][:], in_=cell[t][:], func=ACT.Tanh)
+            nc.sync.dma_start(out=out_rows[1, t], in_=cell[t][:])
+        for t in tiles:
+            nc.vector.tensor_mul(out=hidden[t][:], in0=gate[GATE_O][t][:], in1=cell_tanh[t][:])
+            nc.sync.dma_start(out=out_rows[0, t], in_=hidden[t][:])

@@ -40,7 +40,6 @@ def tile_lstm_s_kernel(tc, pre_layer, x, W_i, W_f, W_o, W_c, U_i, U_f, U_o, U_c,
     with ExitStack() as stack:
         keep = stack.enter_context(tc.tile_pool(name="keep", bufs=1))
         psum = stack.enter_context(tc.psum_pool(name="psum", bufs=PSUM_BANKS))
-        stack.enter_context(tc.manual_schedule())
 
         def unit_tile(name):
             return keep.tile([P, UNITS], F32, name=name)

@@ -40,6 +40,7 @@ def tile_lstm_s_kernel(tc, pre_layer, x, W_i, W_f, W_o, W_c, U_i, U_f, U_o, U_c,
     with ExitStack() as stack:
         keep = stack.enter_context(tc.tile_pool(name="keep", bufs=1))
         psum = stack.enter_context(tc.psum_pool(name="psum", bufs=PSUM_BANKS))
+        stack.enter_context(tc.manual_schedule())
 
         def unit_tile(name):
             return keep.tile([P, UNITS], F32, name=name)
@@ -85,13 +86,17 @@ def tile_lstm_s_kernel(tc, pre_layer, x, W_i, W_f, W_o, W_c, U_i, U_f, U_o, U_c,
                     nc.tensor.transpose(xT_ps[t][:, c, u, :], x_words[:, c, u, :], ident_f32[:])
 
         def regroup_x(t):
-            nc.scalar.copy(
-                out=x_grouped[t][:].bitcast(F32).rearrange("p (c b u) -> p c b u", c=PASSES, u=PAIRS),
-                in_=xT_ps[t][:].rearrange("p c u b -> p c b u"),
-            )
+            grouped_words = x_grouped[t][:].bitcast(F32).rearrange("p (c b u) -> p c b u", c=PASSES, u=PAIRS)
+            for c in range(PASSES):
+                nc.scalar.copy(out=grouped_words[:, c], in_=xT_ps[t][:, c].rearrange("p u b -> p b u"))
 
         def quantise_x(t):
-            nc.vector.quantize_mx(out=x_codes[t][:].bitcast(FP8X4), scales=x_scales[t][:], in_=x_grouped[t][:])
+            for c in range(PASSES):
+                nc.vector.quantize_mx(
+                    out=x_codes[t][:, c * P : (c + 1) * P].bitcast(FP8X4),
+                    scales=x_scales[t][:, c * P : (c + 1) * P],
+                    in_=x_grouped[t][:, c * K_PASS : (c + 1) * K_PASS],
+                )
 
         w_grouped = [
             keep.tile([P, PASSES, UNITS, PACK], BF16, align_bytes=64, name="w_grouped%d" % g) for g in range(GATES)
@@ -111,11 +116,12 @@ def tile_lstm_s_kernel(tc, pre_layer, x, W_i, W_f, W_o, W_c, U_i, U_f, U_o, U_c,
                 )
 
         def quantise_w(g):
-            nc.vector.quantize_mx(
-                out=w_codes[g][:].bitcast(FP8X4),
-                scales=w_scales[g][:],
-                in_=w_grouped[g][:].rearrange("p c w j -> p (c w j)"),
-            )
+            for c in range(PASSES):
+                nc.vector.quantize_mx(
+                    out=w_codes[g][:, c * UNITS : (c + 1) * UNITS].bitcast(FP8X4),
+                    scales=w_scales[g][:, c * UNITS : (c + 1) * UNITS],
+                    in_=w_grouped[g][:, c].rearrange("p w j -> p (w j)"),
+                )
 
         for t in tiles:
             transpose_x(t)

@@ -24,7 +24,7 @@ PSUM_BANKS = 8
 GATE_I, GATE_F, GATE_N, GATE_O = range(4)
 GATES = 4
 
-VECTOR_COLS = 96
+VECTOR_COLS = 112
 RUN = 4
 
 FLOPS = 2 * BATCH * (D_IN + UNITS) * GATES * UNITS

@@ -24,10 +24,24 @@ PSUM_BANKS = 8
 GATE_I, GATE_F, GATE_N, GATE_O = range(4)
 GATES = 4
 
-VECTOR_COLS = 112
+VECTOR_COLS = (128, 128, 128, 128)
 RUN = 4
 
 FLOPS = 2 * BATCH * (D_IN + UNITS) * GATES * UNITS
+
+LOADS = "x0 x1 Wi Wf pre Ui Uf Un Uo Wn Wo"
+ORDER = """
+xT00 xT01 xT10 xT11
+rgVi0 rgVi1 xe00 xe01 qi0 qi1 qx00 qx01
+rgVf0 rgVf1 xe10 xe11 qf0 qf1 qx10 qx11
+hT0 hT1 hTe rec0 rec1
+rgVn0 rgVn1 rgVo0 rgVo1 qn0 qn1 qo0 qo1
+rece0 rece1
+mxi0 addi0 acti0 mxi1 addi1 acti1 mxf0 addf0 actf0 mxf1 addf1 actf1 mxn0 addn0 actn0 mxn1 addn1 actn1
+kept0 kept1 fresh0 fresh1
+mxo0 addo0 acto0 mxo1 addo1 acto1
+cell0 tc0 cell1 tc1 hid0 hid1
+"""
 
 
 def tile_lstm_s_kernel(tc, pre_layer, x, W_i, W_f, W_o, W_c, U_i, U_f, U_o, U_c, out):
@@ -42,157 +56,188 @@ def tile_lstm_s_kernel(tc, pre_layer, x, W_i, W_f, W_o, W_c, U_i, U_f, U_o, U_c,
         psum = stack.enter_context(tc.psum_pool(name="psum", bufs=PSUM_BANKS))
         stack.enter_context(tc.manual_schedule())
 
-        def unit_tile(name):
-            return keep.tile([P, UNITS], F32, name=name)
-
         x_rows = x.rearrange("(p t) k -> t p k", t=B_TILES)
         x_sb = [keep.tile([P, D_IN], BF16, name="x_sb%d" % t) for t in tiles]
         w_raw = [keep.tile([P, PASSES, PACK, UNITS], BF16, name="w_raw%d" % g) for g in range(GATES)]
         pre_sb = keep.tile([P, 2, B_TILES, UNITS], BF16)
         u_sb = keep.tile([P, GATES, UNITS], BF16)
 
-        def load_w(g):
-            nc.sync.dma_start(out=w_raw[g][:], in_=w_dram[g].rearrange("(c p j) w -> p c j w", c=PASSES, j=PACK))
-
-        for t in tiles:
-            nc.sync.dma_start(out=x_sb[t][:], in_=x_rows[t])
-        load_w(GATE_I)
-        load_w(GATE_F)
-        nc.sync.dma_start(out=pre_sb[:], in_=pre_layer.rearrange("s (p t) u -> p s t u", t=B_TILES))
-        for g in range(GATES):
-            nc.sync.dma_start(out=u_sb[:, g, :], in_=u_dram[g])
-        load_w(GATE_N)
-        load_w(GATE_O)
+        for name in LOADS.split():
+            if name[0] == "x":
+                t = int(name[1])
+                nc.sync.dma_start(out=x_sb[t][:], in_=x_rows[t])
+            elif name[0] == "W":
+                g = "ifno".index(name[1])
+                nc.sync.dma_start(out=w_raw[g][:], in_=w_dram[g].rearrange("(c p j) w -> p c j w", c=PASSES, j=PACK))
+            elif name[0] == "U":
+                g = "ifno".index(name[1])
+                nc.sync.dma_start(out=u_sb[:, g, :], in_=u_dram[g])
+            else:
+                nc.sync.dma_start(out=pre_sb[:], in_=pre_layer.rearrange("s (p t) u -> p s t u", t=B_TILES))
 
         ident_f32 = keep.tile([P, P], F32)
         make_identity(nc, ident_f32[:])
         ident_bf16 = keep.tile([P, P], BF16)
         make_identity(nc, ident_bf16[:])
-
         table_in = keep.tile([P, 1], F32)
         table_out = keep.tile([P, 1], F32)
         nc.vector.memset(table_in[:], 0.0)
         nc.scalar.activation(out=table_out[:], in_=table_in[:], func=ACT.Sigmoid)
 
-        xT_ps = [psum.tile([P, PASSES, PAIRS, P], F32, tag="bank", name="xT_ps%d" % t) for t in tiles]
+        banks = {}
+
+        def bank(name, shape, dtype):
+            if name not in banks:
+                banks[name] = psum.tile(shape, dtype, tag="bank", name=name)
+            return banks[name]
+
+        def unit_tile(name):
+            return keep.tile([P, UNITS], F32, name=name)
+
         x_grouped = [keep.tile([P, PASSES * P * PACK], BF16, align_bytes=64, name="x_grouped%d" % t) for t in tiles]
         x_codes = [keep.tile([P, PASSES * P], U32, align_bytes=64, name="x_codes%d" % t) for t in tiles]
         x_scales = [keep.tile([P, PASSES * P], U8, align_bytes=64, name="x_scales%d" % t) for t in tiles]
-
-        def transpose_x(t):
-            x_words = x_sb[t][:].bitcast(F32).rearrange("p (c q u) -> p c u q", c=PASSES, u=PAIRS)
-            for c in range(PASSES):
-                for u in range(PAIRS):
-                    nc.tensor.transpose(xT_ps[t][:, c, u, :], x_words[:, c, u, :], ident_f32[:])
-
-        def regroup_x(t):
-            grouped_words = x_grouped[t][:].bitcast(F32).rearrange("p (c b u) -> p c b u", c=PASSES, u=PAIRS)
-            for c in range(PASSES):
-                nc.scalar.copy(out=grouped_words[:, c], in_=xT_ps[t][:, c].rearrange("p u b -> p b u"))
-
-        def quantise_x(t):
-            for c in range(PASSES):
-                nc.vector.quantize_mx(
-                    out=x_codes[t][:, c * P : (c + 1) * P].bitcast(FP8X4),
-                    scales=x_scales[t][:, c * P : (c + 1) * P],
-                    in_=x_grouped[t][:, c * K_PASS : (c + 1) * K_PASS],
-                )
-
         w_grouped = [
             keep.tile([P, PASSES, UNITS, PACK], BF16, align_bytes=64, name="w_grouped%d" % g) for g in range(GATES)
         ]
         w_codes = [keep.tile([P, PASSES * UNITS], U32, align_bytes=64, name="w_codes%d" % g) for g in range(GATES)]
         w_scales = [keep.tile([P, PASSES * UNITS], U8, align_bytes=64, name="w_scales%d" % g) for g in range(GATES)]
-
-        def regroup_w(g):
-            for c in range(PASSES):
-                nc.vector.tensor_copy(
-                    out=w_grouped[g][:, c, :VECTOR_COLS, :].rearrange("p (a i) j -> p a j i", i=RUN),
-                    in_=w_raw[g][:, c, :, :VECTOR_COLS].rearrange("p j (a i) -> p a j i", i=RUN),
-                )
-                nc.scalar.copy(
-                    out=w_grouped[g][:, c, VECTOR_COLS:, :].rearrange("p (a i) j -> p a j i", i=RUN),
-                    in_=w_raw[g][:, c, :, VECTOR_COLS:].rearrange("p j (a i) -> p a j i", i=RUN),
-                )
-
-        def quantise_w(g):
-            for c in range(PASSES):
-                nc.vector.quantize_mx(
-                    out=w_codes[g][:, c * UNITS : (c + 1) * UNITS].bitcast(FP8X4),
-                    scales=w_scales[g][:, c * UNITS : (c + 1) * UNITS],
-                    in_=w_grouped[g][:, c].rearrange("p w j -> p (w j)"),
-                )
-
-        for t in tiles:
-            transpose_x(t)
-        for t, g in zip(tiles, (GATE_I, GATE_F)):
-            regroup_w(g)
-            regroup_x(t)
-            quantise_w(g)
-            quantise_x(t)
-
-        hT_ps = psum.tile([P, B_TILES, P], BF16, tag="bank")
-        for t in tiles:
-            nc.tensor.transpose(hT_ps[:, t, :], pre_sb[:, 0, t, :], ident_bf16[:])
         hT_sb = keep.tile([P, B_TILES, P], BF16)
-        nc.scalar.copy(out=hT_sb[:], in_=hT_ps[:])
-        rec_ps = [psum.tile([P, GATES * UNITS], F32, tag="bank", name="rec_ps%d" % t) for t in tiles]
-        for t in tiles:
+        rec_sb = [keep.tile([P, GATES, UNITS], F32, name="rec_sb%d" % t) for t in tiles]
+        z = [[unit_tile("z%d_%d" % (g, t)) for t in tiles] for g in range(GATES)]
+        gate = [[unit_tile("gate%d_%d" % (g, t)) for t in tiles] for g in range(GATES)]
+        kept = [unit_tile("kept%d" % t) for t in tiles]
+        fresh = [unit_tile("fresh%d" % t) for t in tiles]
+        cell = [unit_tile("cell%d" % t) for t in tiles]
+        cell_tanh = [unit_tile("cell_tanh%d" % t) for t in tiles]
+        hidden = [unit_tile("hidden%d" % t) for t in tiles]
+        out_rows = out.rearrange("s (p t) u -> s t p u", t=B_TILES)
+
+        def xT_ps(t):
+            return bank("xT_ps%d" % t, [P, PASSES, PAIRS, P], F32)
+
+        def hT_ps():
+            return bank("hT_ps", [P, B_TILES, P], BF16)
+
+        def rec_ps(t):
+            return bank("rec_ps%d" % t, [P, GATES * UNITS], F32)
+
+        def acc_ps(g, t):
+            return bank("acc%d_%d" % (g, t), [P, UNITS], F32)
+
+        def transpose_x(t, c):
+            x_words = x_sb[t][:].bitcast(F32).rearrange("p (c q u) -> p c u q", c=PASSES, u=PAIRS)
+            for u in range(PAIRS):
+                nc.tensor.transpose(xT_ps(t)[:, c, u, :], x_words[:, c, u, :], ident_f32[:])
+
+        def regroup_x(t, c):
+            grouped_words = x_grouped[t][:].bitcast(F32).rearrange("p (c b u) -> p c b u", c=PASSES, u=PAIRS)
+            nc.scalar.copy(out=grouped_words[:, c], in_=xT_ps(t)[:, c].rearrange("p u b -> p b u"))
+
+        def quantise_x(t, c):
+            nc.vector.quantize_mx(
+                out=x_codes[t][:, c * P : (c + 1) * P].bitcast(FP8X4),
+                scales=x_scales[t][:, c * P : (c + 1) * P],
+                in_=x_grouped[t][:, c * K_PASS : (c + 1) * K_PASS],
+            )
+
+        def regroup_w(g, c, copy, cols):
+            copy(
+                out=w_grouped[g][:, c, cols, :].rearrange("p (a i) j -> p a j i", i=RUN),
+                in_=w_raw[g][:, c, :, cols].rearrange("p j (a i) -> p a j i", i=RUN),
+            )
+
+        def quantise_w(g, c):
+            nc.vector.quantize_mx(
+                out=w_codes[g][:, c * UNITS : (c + 1) * UNITS].bitcast(FP8X4),
+                scales=w_scales[g][:, c * UNITS : (c + 1) * UNITS],
+                in_=w_grouped[g][:, c].rearrange("p w j -> p (w j)"),
+            )
+
+        def transpose_h(t):
+            nc.tensor.transpose(hT_ps()[:, t, :], pre_sb[:, 0, t, :], ident_bf16[:])
+
+        def copy_h():
+            nc.scalar.copy(out=hT_sb[:], in_=hT_ps()[:])
+
+        def recurrent(t):
             nc.tensor.matmul(
-                out=rec_ps[t][:],
+                out=rec_ps(t)[:],
                 lhsT=hT_sb[:, t, :],
                 rhs=u_sb[:].rearrange("p g u -> p (g u)"),
                 start=True,
                 stop=True,
             )
 
-        for g in (GATE_N, GATE_O):
-            regroup_w(g)
-        for g in (GATE_N, GATE_O):
-            quantise_w(g)
+        def copy_recurrent(t):
+            nc.scalar.copy(out=rec_sb[t][:].rearrange("p g u -> p (g u)"), in_=rec_ps(t)[:])
 
-        rec_sb = [keep.tile([P, GATES, UNITS], F32, name="rec_sb%d" % t) for t in tiles]
-        for t in tiles:
-            nc.scalar.copy(out=rec_sb[t][:].rearrange("p g u -> p (g u)"), in_=rec_ps[t][:])
+        def product(g, t):
+            for c in range(PASSES):
+                cols = slice(c * P, (c + 1) * P)
+                nc.tensor.matmul_mx(
+                    out=acc_ps(g, t)[:],
+                    lhsT=x_codes[t][:, cols].bitcast(FP8X4),
+                    lhsT_scale=x_scales[t][:, cols],
+                    rhs=w_codes[g][:, cols].bitcast(FP8X4),
+                    rhs_scale=w_scales[g][:, cols],
+                    start=(c == 0),
+                    stop=(c == PASSES - 1),
+                )
 
-        gate = [[unit_tile("gate%d_%d" % (g, t)) for t in tiles] for g in range(GATES)]
+        def add_gate(g, t):
+            nc.vector.tensor_add(out=z[g][t][:], in0=acc_ps(g, t)[:], in1=rec_sb[t][:, g, :])
 
-        def compute_gate(g):
-            for t in tiles:
-                acc = psum.tile([P, UNITS], F32, tag="bank", name="acc%d_%d" % (g, t))
-                for c in range(PASSES):
-                    cols = slice(c * P, (c + 1) * P)
-                    nc.tensor.matmul_mx(
-                        out=acc[:],
-                        lhsT=x_codes[t][:, cols].bitcast(FP8X4),
-                        lhsT_scale=x_scales[t][:, cols],
-                        rhs=w_codes[g][:, cols].bitcast(FP8X4),
-                        rhs_scale=w_scales[g][:, cols],
-                        start=(c == 0),
-                        stop=(c == PASSES - 1),
-                    )
-                z = unit_tile("z%d_%d" % (g, t))
-                nc.vector.tensor_add(out=z[:], in0=acc[:], in1=rec_sb[t][:, g, :])
-                nc.scalar.activation(out=gate[g][t][:], in_=z[:], func=gate_func[g])
+        def act_gate(g, t):
+            nc.scalar.activation(out=gate[g][t][:], in_=z[g][t][:], func=gate_func[g])
 
-        for g in (GATE_I, GATE_F, GATE_N):
-            compute_gate(g)
-
-        out_rows = out.rearrange("s (p t) u -> s t p u", t=B_TILES)
-        kept = [unit_tile("kept%d" % t) for t in tiles]
-        fresh = [unit_tile("fresh%d" % t) for t in tiles]
-        cell = [unit_tile("cell%d" % t) for t in tiles]
-        cell_tanh = [unit_tile("cell_tanh%d" % t) for t in tiles]
-        hidden = [unit_tile("hidden%d" % t) for t in tiles]
-        for t in tiles:
+        def keep_old(t):
             nc.vector.tensor_mul(out=kept[t][:], in0=gate[GATE_F][t][:], in1=pre_sb[:, 1, t, :])
-        for t in tiles:
+
+        def take_new(t):
             nc.vector.tensor_mul(out=fresh[t][:], in0=gate[GATE_I][t][:], in1=gate[GATE_N][t][:])
-        compute_gate(GATE_O)
-        for t in tiles:
+
+        def new_cell(t):
             nc.vector.tensor_add(out=cell[t][:], in0=kept[t][:], in1=fresh[t][:])
-            nc.scalar.activation(out=cell_tanh[t][:], in_=cell[t][:], func=ACT.Tanh)
             nc.sync.dma_start(out=out_rows[1, t], in_=cell[t][:])
-        for t in tiles:
+
+        def squash_cell(t):
+            nc.scalar.activation(out=cell_tanh[t][:], in_=cell[t][:], func=ACT.Tanh)
+
+        def new_hidden(t):
             nc.vector.tensor_mul(out=hidden[t][:], in0=gate[GATE_O][t][:], in1=cell_tanh[t][:])
             nc.sync.dma_start(out=out_rows[0, t], in_=hidden[t][:])
+
+        def bind(f, *args):
+            return lambda: f(*args)
+
+        steps = {"hTe": copy_h}
+        for t in tiles:
+            s = str(t)
+            steps["hT" + s] = bind(transpose_h, t)
+            steps["rec" + s] = bind(recurrent, t)
+            steps["rece" + s] = bind(copy_recurrent, t)
+            steps["kept" + s] = bind(keep_old, t)
+            steps["fresh" + s] = bind(take_new, t)
+            steps["cell" + s] = bind(new_cell, t)
+            steps["tc" + s] = bind(squash_cell, t)
+            steps["hid" + s] = bind(new_hidden, t)
+            for c in range(PASSES):
+                steps["xT" + s + str(c)] = bind(transpose_x, t, c)
+                steps["xe" + s + str(c)] = bind(regroup_x, t, c)
+                steps["qx" + s + str(c)] = bind(quantise_x, t, c)
+        for g, name in enumerate("ifno"):
+            for c in range(PASSES):
+                if VECTOR_COLS[g] > 0:
+                    steps["rgV" + name + str(c)] = bind(regroup_w, g, c, nc.vector.tensor_copy, slice(0, VECTOR_COLS[g]))
+                if VECTOR_COLS[g] < UNITS:
+                    steps["rgS" + name + str(c)] = bind(regroup_w, g, c, nc.scalar.copy, slice(VECTOR_COLS[g], UNITS))
+                steps["q" + name + str(c)] = bind(quantise_w, g, c)
+            for t in tiles:
+                steps["mx" + name + str(t)] = bind(product, g, t)
+                steps["add" + name + str(t)] = bind(add_gate, g, t)
+                steps["act" + name + str(t)] = bind(act_gate, g, t)
+
+        for name in ORDER.split():
+            steps[name]()
+        assert len(ORDER.split()) == len(steps)

@@ -29,11 +29,11 @@ RUN = 4
 
 FLOPS = 2 * BATCH * (D_IN + UNITS) * GATES * UNITS
 
-LOADS = "x0 x1 Wi Wf pre Ui Uf Un Uo Wn Wo"
+LOADS = "x0 Wi x1 Wf pre Ui Uf Un Uo Wn Wo"
 ORDER = """
 xT00 xT01 xT10 xT11
-rgVi0 rgVi1 xe00 xe01 qi0 qi1 qx00 qx01
-rgVf0 rgVf1 xe10 xe11 qf0 qf1 qx10 qx11
+rgVi0 rgVi1 xe00 xe01 qi0 qi1 qx00
+rgVf0 rgVf1 qx01 xe10 xe11 qf0 qf1 qx10 qx11
 hT0 hT1 hTe rec0 rec1
 rgVn0 rgVn1 rgVo0 rgVo1 qn0 qn1 qo0 qo1
 rece0 rece1
@@ -63,9 +63,19 @@ def tile_lstm_s_kernel(tc, pre_layer, x, W_i, W_f, W_o, W_c, U_i, U_f, U_o, U_c,
         u_sb = keep.tile([P, GATES, UNITS], BF16)
 
         for name in LOADS.split():
-            if name[0] == "x":
+            if name[0] == "x" and len(name) == 3:
+                t = int(name[1])
+                half = slice(int(name[2]) * K_PASS, (int(name[2]) + 1) * K_PASS)
+                nc.sync.dma_start(out=x_sb[t][:, half], in_=x_rows[t][:, half])
+            elif name[0] == "x":
                 t = int(name[1])
                 nc.sync.dma_start(out=x_sb[t][:], in_=x_rows[t])
+            elif name[0] == "W" and len(name) == 3:
+                g = "ifno".index(name[1])
+                c = int(name[2])
+                nc.sync.dma_start(
+                    out=w_raw[g][:, c], in_=w_dram[g].rearrange("(c p j) w -> c p j w", c=PASSES, j=PACK)[c]
+                )
             elif name[0] == "W":
                 g = "ifno".index(name[1])
                 nc.sync.dma_start(out=w_raw[g][:], in_=w_dram[g].rearrange("(c p j) w -> p c j w", c=PASSES, j=PACK))

@@ -21,34 +21,38 @@ PASSES = D_IN // K_PASS
 B_TILES = BATCH // P
 PSUM_BANKS = 8
 
-GATE_I, GATE_F, GATE_N, GATE_O = range(4)
+GATE_I, GATE_N, GATE_F, GATE_O = range(4)
 GATES = 4
+HALF_GATES = 2
 
 VECTOR_COLS = (128, 128, 128, 128)
 RUN = 4
 
 FLOPS = 2 * BATCH * (D_IN + UNITS) * GATES * UNITS
 
-LOADS = "x0 Wi x1 Wf pre Ui Uf Un Uo Wn Wo"
+LOADS = "x0 Wi Wf ph x1 Un Ui Wn Uo Uf Wo pc"
 ORDER = """
-xT00 xT01 xT10 xT11
-rgVi0 rgVi1 xe00 xe01 qi0 qi1 qx00
-rgVf0 rgVf1 qx01 xe10 xe11 qf0 qf1 qx10 qx11
-hT0 hT1 hTe rec0 rec1
-rgVn0 rgVn1 rgVo0 rgVo1 qn0 qn1 qo0 qo1
-rece0 rece1
-mxi0 addi0 acti0 mxi1 addi1 acti1 mxf0 addf0 actf0 mxf1 addf1 actf1 mxn0 addn0 actn0 mxn1 addn1 actn1
-kept0 kept1 fresh0 fresh1
-mxo0 addo0 acto0 mxo1 addo1 acto1
-cell0 tc0 cell1 tc1 hid0 hid1
+xT00 xT01 hT0 hT1 xT10 xT11
+xe00 xe01 hTe xe10 xe11
+rgVi0 rgVi1 qi0 rgVf0 qx00 rgVf1 qi1 qx01 qf0 qf1
+rgVn0 rgVn1 qx10 qx11 qn0 qn1
+rec0a rec1a rec0b rec1b
+rece0a rece1a rece0b rece1b
+mxi0 mxi1 mxf0 mxf1 mxn0 mxn1
+rgVo0 addi0 rgVo1 addi1 addf0 addf1 addn0 addn1
+acti0 acti1 actf0 actf1 actn0 actn1
+qo0 qo1 mxo0 mxo1
+kept0 kept1 fresh0 fresh1 cell0 cell1 addo0 addo1
+tc0 tc1 acto0 acto1
+hid0 hid1
 """
 
 
 def tile_lstm_s_kernel(tc, pre_layer, x, W_i, W_f, W_o, W_c, U_i, U_f, U_o, U_c, out):
     nc = tc.nc
-    w_dram = (W_i, W_f, W_c, W_o)
-    u_dram = (U_i, U_f, U_c, U_o)
-    gate_func = (ACT.Sigmoid, ACT.Sigmoid, ACT.Tanh, ACT.Sigmoid)
+    w_dram = (W_i, W_c, W_f, W_o)
+    u_dram = (U_i, U_c, U_f, U_o)
+    gate_func = (ACT.Sigmoid, ACT.Tanh, ACT.Sigmoid, ACT.Sigmoid)
     tiles = range(B_TILES)
 
     with ExitStack() as stack:
@@ -59,7 +63,7 @@ def tile_lstm_s_kernel(tc, pre_layer, x, W_i, W_f, W_o, W_c, U_i, U_f, U_o, U_c,
         x_rows = x.rearrange("(p t) k -> t p k", t=B_TILES)
         x_sb = [keep.tile([P, D_IN], BF16, name="x_sb%d" % t) for t in tiles]
         w_raw = [keep.tile([P, PASSES, PACK, UNITS], BF16, name="w_raw%d" % g) for g in range(GATES)]
-        pre_sb = keep.tile([P, 2, B_TILES, UNITS], BF16)
+        pre_sb = [keep.tile([P, B_TILES, UNITS], BF16, name="pre_sb%d" % s) for s in range(2)]
         u_sb = keep.tile([P, GATES, UNITS], BF16)
 
         for name in LOADS.split():
@@ -71,19 +75,20 @@ def tile_lstm_s_kernel(tc, pre_layer, x, W_i, W_f, W_o, W_c, U_i, U_f, U_o, U_c,
                 t = int(name[1])
                 nc.sync.dma_start(out=x_sb[t][:], in_=x_rows[t])
             elif name[0] == "W" and len(name) == 3:
-                g = "ifno".index(name[1])
+                g = "info".index(name[1])
                 c = int(name[2])
                 nc.sync.dma_start(
                     out=w_raw[g][:, c], in_=w_dram[g].rearrange("(c p j) w -> c p j w", c=PASSES, j=PACK)[c]
                 )
             elif name[0] == "W":
-                g = "ifno".index(name[1])
+                g = "info".index(name[1])
                 nc.sync.dma_start(out=w_raw[g][:], in_=w_dram[g].rearrange("(c p j) w -> p c j w", c=PASSES, j=PACK))
             elif name[0] == "U":
-                g = "ifno".index(name[1])
+                g = "info".index(name[1])
                 nc.sync.dma_start(out=u_sb[:, g, :], in_=u_dram[g])
             else:
-                nc.sync.dma_start(out=pre_sb[:], in_=pre_layer.rearrange("s (p t) u -> p s t u", t=B_TILES))
+                s = "hc".index(name[1])
+                nc.sync.dma_start(out=pre_sb[s][:], in_=pre_layer.rearrange("s (p t) u -> s p t u", t=B_TILES)[s])
 
         ident_f32 = keep.tile([P, P], F32)
         make_identity(nc, ident_f32[:])
@@ -123,14 +128,14 @@ def tile_lstm_s_kernel(tc, pre_layer, x, W_i, W_f, W_o, W_c, U_i, U_f, U_o, U_c,
         hidden = [unit_tile("hidden%d" % t) for t in tiles]
         out_rows = out.rearrange("s (p t) u -> s t p u", t=B_TILES)
 
-        def xT_ps(t):
-            return bank("xT_ps%d" % t, [P, PASSES, PAIRS, P], F32)
+        def xT_ps(t, c):
+            return bank("xT_ps%d_%d" % (t, c), [P, PAIRS, P], F32)
 
         def hT_ps():
             return bank("hT_ps", [P, B_TILES, P], BF16)
 
-        def rec_ps(t):
-            return bank("rec_ps%d" % t, [P, GATES * UNITS], F32)
+        def rec_ps(t, h):
+            return bank("rec_ps%d_%d" % (t, h), [P, HALF_GATES * UNITS], F32)
 
         def acc_ps(g, t):
             return bank("acc%d_%d" % (g, t), [P, UNITS], F32)
@@ -138,11 +143,11 @@ def tile_lstm_s_kernel(tc, pre_layer, x, W_i, W_f, W_o, W_c, U_i, U_f, U_o, U_c,
         def transpose_x(t, c):
             x_words = x_sb[t][:].bitcast(F32).rearrange("p (c q u) -> p c u q", c=PASSES, u=PAIRS)
             for u in range(PAIRS):
-                nc.tensor.transpose(xT_ps(t)[:, c, u, :], x_words[:, c, u, :], ident_f32[:])
+                nc.tensor.transpose(xT_ps(t, c)[:, u, :], x_words[:, c, u, :], ident_f32[:])
 
         def regroup_x(t, c):
             grouped_words = x_grouped[t][:].bitcast(F32).rearrange("p (c b u) -> p c b u", c=PASSES, u=PAIRS)
-            nc.scalar.copy(out=grouped_words[:, c], in_=xT_ps(t)[:, c].rearrange("p u b -> p b u"))
+            nc.scalar.copy(out=grouped_words[:, c], in_=xT_ps(t, c)[:].rearrange("p u b -> p b u"))
 
         def quantise_x(t, c):
             nc.vector.quantize_mx(
@@ -165,22 +170,25 @@ def tile_lstm_s_kernel(tc, pre_layer, x, W_i, W_f, W_o, W_c, U_i, U_f, U_o, U_c,
             )
 
         def transpose_h(t):
-            nc.tensor.transpose(hT_ps()[:, t, :], pre_sb[:, 0, t, :], ident_bf16[:])
+            nc.tensor.transpose(hT_ps()[:, t, :], pre_sb[0][:, t, :], ident_bf16[:])
 
         def copy_h():
             nc.scalar.copy(out=hT_sb[:], in_=hT_ps()[:])
 
-        def recurrent(t):
+        def half(h):
+            return slice(h * HALF_GATES, (h + 1) * HALF_GATES)
+
+        def recurrent(t, h):
             nc.tensor.matmul(
-                out=rec_ps(t)[:],
+                out=rec_ps(t, h)[:],
                 lhsT=hT_sb[:, t, :],
-                rhs=u_sb[:].rearrange("p g u -> p (g u)"),
+                rhs=u_sb[:, half(h), :].rearrange("p g u -> p (g u)"),
                 start=True,
                 stop=True,
             )
 
-        def copy_recurrent(t):
-            nc.scalar.copy(out=rec_sb[t][:].rearrange("p g u -> p (g u)"), in_=rec_ps(t)[:])
+        def copy_recurrent(t, h):
+            nc.scalar.copy(out=rec_sb[t][:, half(h), :].rearrange("p g u -> p (g u)"), in_=rec_ps(t, h)[:])
 
         def product(g, t):
             for c in range(PASSES):
@@ -202,7 +210,7 @@ def tile_lstm_s_kernel(tc, pre_layer, x, W_i, W_f, W_o, W_c, U_i, U_f, U_o, U_c,
             nc.scalar.activation(out=gate[g][t][:], in_=z[g][t][:], func=gate_func[g])
 
         def keep_old(t):
-            nc.vector.tensor_mul(out=kept[t][:], in0=gate[GATE_F][t][:], in1=pre_sb[:, 1, t, :])
+            nc.vector.tensor_mul(out=kept[t][:], in0=gate[GATE_F][t][:], in1=pre_sb[1][:, t, :])
 
         def take_new(t):
             nc.vector.tensor_mul(out=fresh[t][:], in0=gate[GATE_I][t][:], in1=gate[GATE_N][t][:])
@@ -225,8 +233,9 @@ def tile_lstm_s_kernel(tc, pre_layer, x, W_i, W_f, W_o, W_c, U_i, U_f, U_o, U_c,
         for t in tiles:
             s = str(t)
             steps["hT" + s] = bind(transpose_h, t)
-            steps["rec" + s] = bind(recurrent, t)
-            steps["rece" + s] = bind(copy_recurrent, t)
+            for h, name in enumerate("ab"):
+                steps["rec" + s + name] = bind(recurrent, t, h)
+                steps["rece" + s + name] = bind(copy_recurrent, t, h)
             steps["kept" + s] = bind(keep_old, t)
             steps["fresh" + s] = bind(take_new, t)
             steps["cell" + s] = bind(new_cell, t)
@@ -236,7 +245,7 @@ def tile_lstm_s_kernel(tc, pre_layer, x, W_i, W_f, W_o, W_c, U_i, U_f, U_o, U_c,
                 steps["xT" + s + str(c)] = bind(transpose_x, t, c)
                 steps["xe" + s + str(c)] = bind(regroup_x, t, c)
                 steps["qx" + s + str(c)] = bind(quantise_x, t, c)
-        for g, name in enumerate("ifno"):
+        for g, name in enumerate("info"):
             for c in range(PASSES):
                 if VECTOR_COLS[g] > 0:
                     steps["rgV" + name + str(c)] = bind(regroup_w, g, c, nc.vector.tensor_copy, slice(0, VECTOR_COLS[g]))

@@ -30,20 +30,21 @@ RUN = 4
 
 FLOPS = 2 * BATCH * (D_IN + UNITS) * GATES * UNITS
 
-LOADS = "x0 Wi Wf ph x1 Un Ui Wn Uo Uf Wo pc"
+LOADS = "Wi x0 Wf ph x1 Wn Un Ui Wo Uo Uf pc"
 ORDER = """
 xT00 xT01 hT0 hT1 xT10 xT11
+rgVi0 rgVi1 qi0 qi1 rgVf0 rgVf1
 xe00 xe01 hTe xe10 xe11
-rgVi0 rgVi1 qi0 rgVf0 qx00 rgVf1 qi1 qx01 qf0 qf1
-rgVn0 rgVn1 qx10 qx11 qn0 qn1
-rec0a rec1a rec0b rec1b
+qf0 qx00 qf1 qx01
+rgVn0 rgVn1 qn0 qx10 qn1 qx11
+rec0a rec1a mxi0 mxf0 rec0b rec1b mxn0 mxi1 mxf1 mxn1
 rece0a rece1a rece0b rece1b
-mxi0 mxi1 mxf0 mxf1 mxn0 mxn1
-rgVo0 addi0 rgVo1 addi1 addf0 addf1 addn0 addn1
-acti0 acti1 actf0 actf1 actn0 actn1
-qo0 qo1 mxo0 mxo1
-kept0 kept1 fresh0 fresh1 cell0 cell1 addo0 addo1
-tc0 tc1 acto0 acto1
+rgVo0 rgVo1 addi0 qo0 addn0 qo1
+mxo0 mxo1
+addf0 addi1 addn1 addf1
+acti0 actn0 actf0 acti1 actn1 actf1
+fresh0 kept0 fresh1 cell0 kept1 addo0 cell1 addo1
+tc0 acto0 tc1 acto1
 hid0 hid1
 """
 

@@ -30,21 +30,22 @@ RUN = 4
 
 FLOPS = 2 * BATCH * (D_IN + UNITS) * GATES * UNITS
 
-LOADS = "Wi x0 Wf ph x1 Wn Un Ui Wo Uo Uf pc"
+LOADS = "Wi x0 Wf ph x1 Wn Un Ui Uf Uo Wo pc"
 ORDER = """
 xT00 xT01 hT0 hT1 xT10 xT11
 rgVi0 rgVi1 qi0 qi1 rgVf0 rgVf1
 xe00 xe01 hTe xe10 xe11
 qf0 qx00 qf1 qx01
 rgVn0 rgVn1 qn0 qx10 qn1 qx11
-rec0a rec1a mxi0 mxf0 rec0b rec1b mxn0 mxi1 mxf1 mxn1
+rec0a rec1a rec0b rec1b
 rece0a rece1a rece0b rece1b
-rgVo0 rgVo1 addi0 qo0 addn0 qo1
+mxi0 mxf0 mxn0 mxi1 mxf1 mxn1
+rgVo0 rgVo1 addi0 qo0 addf0 addn0 qo1
 mxo0 mxo1
-addf0 addi1 addn1 addf1
-acti0 actn0 actf0 acti1 actn1 actf1
-fresh0 kept0 fresh1 cell0 kept1 addo0 cell1 addo1
-tc0 acto0 tc1 acto1
+addi1 addf1 addn1
+acti0 actf0 actn0 acti1 actf1 actn1
+kept0 fresh0 addo0 cell0 kept1 fresh1 addo1 cell1
+acto0 tc0 acto1 tc1
 hid0 hid1
 """
 

@@ -23,28 +23,28 @@ PSUM_BANKS = 8
 
 GATE_I, GATE_N, GATE_F, GATE_O = range(4)
 GATES = 4
-HALF_GATES = 2
+REC_PARTS = (slice(0, 3), slice(3, 4))
 
 VECTOR_COLS = (128, 128, 128, 128)
 RUN = 4
 
 FLOPS = 2 * BATCH * (D_IN + UNITS) * GATES * UNITS
 
-LOADS = "Wi x0 Wf ph x1 Wn Un Ui Uf Uo Wo pc"
+LOADS = "Wi x0 Wf ph x1 Wn Un Ui Uf Wo Uo pc"
 ORDER = """
 xT00 xT01 hT0 hT1 xT10 xT11
 rgVi0 rgVi1 qi0 qi1 rgVf0 rgVf1
 xe00 xe01 hTe xe10 xe11
 qf0 qx00 qf1 qx01
+mxi0 rec0a rec1a rece0a rece1a
 rgVn0 rgVn1 qn0 qx10 qn1 qx11
-rec0a rec1a rec0b rec1b
-rece0a rece1a rece0b rece1b
-mxi0 mxf0 mxn0 mxi1 mxf1 mxn1
-rgVo0 rgVo1 addi0 qo0 addf0 addn0 qo1
+mxf0 mxn0 mxi1 mxf1 mxn1
+rgVo0 rgVo1 addi0 qo0 addf0 addn0 qo1 addi1 addf1 addn1
+acti0 actf0 actn0
+rec0b rec1b rece0b
+acti1 actf1 actn1 rece1b
 mxo0 mxo1
-addi1 addf1 addn1
-acti0 actf0 actn0 acti1 actf1 actn1
-kept0 fresh0 addo0 cell0 kept1 fresh1 addo1 cell1
+kept0 fresh0 addo0 kept1 fresh1 cell0 addo1 cell1
 acto0 tc0 acto1 tc1
 hid0 hid1
 """
@@ -137,7 +137,7 @@ def tile_lstm_s_kernel(tc, pre_layer, x, W_i, W_f, W_o, W_c, U_i, U_f, U_o, U_c,
             return bank("hT_ps", [P, B_TILES, P], BF16)
 
         def rec_ps(t, h):
-            return bank("rec_ps%d_%d" % (t, h), [P, HALF_GATES * UNITS], F32)
+            return bank("rec_ps%d_%d" % (t, h), [P, (REC_PARTS[h].stop - REC_PARTS[h].start) * UNITS], F32)
 
         def acc_ps(g, t):
             return bank("acc%d_%d" % (g, t), [P, UNITS], F32)
@@ -177,20 +177,17 @@ def tile_lstm_s_kernel(tc, pre_layer, x, W_i, W_f, W_o, W_c, U_i, U_f, U_o, U_c,
         def copy_h():
             nc.scalar.copy(out=hT_sb[:], in_=hT_ps()[:])
 
-        def half(h):
-            return slice(h * HALF_GATES, (h + 1) * HALF_GATES)
-
         def recurrent(t, h):
             nc.tensor.matmul(
                 out=rec_ps(t, h)[:],
                 lhsT=hT_sb[:, t, :],
-                rhs=u_sb[:, half(h), :].rearrange("p g u -> p (g u)"),
+                rhs=u_sb[:, REC_PARTS[h], :].rearrange("p g u -> p (g u)"),
                 start=True,
                 stop=True,
             )
 
         def copy_recurrent(t, h):
-            nc.scalar.copy(out=rec_sb[t][:, half(h), :].rearrange("p g u -> p (g u)"), in_=rec_ps(t, h)[:])
+            nc.scalar.copy(out=rec_sb[t][:, REC_PARTS[h], :].rearrange("p g u -> p (g u)"), in_=rec_ps(t, h)[:])
 
         def product(g, t):
             for c in range(PASSES):

@@ -38,12 +38,12 @@ xe00 xe01 hTe xe10 xe11
 qf0 qx00 qf1 qx01
 mxi0 rec0a rec1a rece0a rece1a
 rgVn0 rgVn1 qn0 qx10 qn1 qx11
-mxf0 mxn0 mxi1 mxf1 mxn1
-rgVo0 rgVo1 addi0 qo0 addf0 addn0 qo1 addi1 addf1 addn1
-acti0 actf0 actn0
-rec0b rec1b rece0b
-acti1 actf1 actn1 rece1b
+mxf0 mxn0 rec0b rec1b rece0b rece1b
+mxi1 mxf1 mxn1
+rgVo0 rgVo1 qo0 addi0 qo1
 mxo0 mxo1
+addf0 addn0 addi1 addf1 addn1
+acti0 actf0 actn0 acti1 actf1 actn1
 kept0 fresh0 addo0 kept1 fresh1 cell0 addo1 cell1
 acto0 tc0 acto1 tc1
 hid0 hid1

from contextlib import ExitStack

import concourse.mybir as mybir
from concourse.masks import make_identity

F32 = mybir.dt.float32
BF16 = mybir.dt.bfloat16
U32 = mybir.dt.uint32
U8 = mybir.dt.uint8
FP8X4 = mybir.dt.float8_e4m3fn_x4
ACT = mybir.ActivationFunctionType

P = 128
BATCH = 256
D_IN = 1024
UNITS = 128
PACK = 4
PAIRS = PACK // 2
K_PASS = P * PACK
PASSES = D_IN // K_PASS
B_TILES = BATCH // P
PSUM_BANKS = 8

GATE_I, GATE_N, GATE_F, GATE_O = range(4)
GATES = 4
REC_PARTS = (slice(0, 3), slice(3, 4))

VECTOR_COLS = (128, 128, 128, 128)
RUN = 4

FLOPS = 2 * BATCH * (D_IN + UNITS) * GATES * UNITS

LOADS = "Wi x0 Wf ph x1 Wn Un Ui Uf Wo Uo pc"
ORDER = """
xT00 xT01 hT0 hT1 xT10 xT11
rgVi0 rgVi1 qi0 qi1 rgVf0 rgVf1
xe00 xe01 hTe xe10 xe11
qf0 qx00 qf1 qx01
mxi0 rec0a rec1a rece0a rece1a
rgVn0 rgVn1 qn0 qx10 qn1 qx11
mxf0 mxn0 rec0b rec1b rece0b rece1b
mxi1 mxf1 mxn1
rgVo0 rgVo1 qo0 addi0 qo1
mxo0 mxo1
addf0 addn0 addi1 addf1 addn1
acti0 actf0 actn0 acti1 actf1 actn1
kept0 fresh0 addo0 kept1 fresh1 cell0 addo1 cell1
acto0 tc0 acto1 tc1
hid0 hid1
"""


def tile_lstm_s_kernel(tc, pre_layer, x, W_i, W_f, W_o, W_c, U_i, U_f, U_o, U_c, out):
    nc = tc.nc
    w_dram = (W_i, W_c, W_f, W_o)
    u_dram = (U_i, U_c, U_f, U_o)
    gate_func = (ACT.Sigmoid, ACT.Tanh, ACT.Sigmoid, ACT.Sigmoid)
    tiles = range(B_TILES)

    with ExitStack() as stack:
        keep = stack.enter_context(tc.tile_pool(name="keep", bufs=1))
        psum = stack.enter_context(tc.psum_pool(name="psum", bufs=PSUM_BANKS))
        stack.enter_context(tc.manual_schedule())

        x_rows = x.rearrange("(p t) k -> t p k", t=B_TILES)
        x_sb = [keep.tile([P, D_IN], BF16, name="x_sb%d" % t) for t in tiles]
        w_raw = [keep.tile([P, PASSES, PACK, UNITS], BF16, name="w_raw%d" % g) for g in range(GATES)]
        pre_sb = [keep.tile([P, B_TILES, UNITS], BF16, name="pre_sb%d" % s) for s in range(2)]
        u_sb = keep.tile([P, GATES, UNITS], BF16)

        for name in LOADS.split():
            if name[0] == "x" and len(name) == 3:
                t = int(name[1])
                half = slice(int(name[2]) * K_PASS, (int(name[2]) + 1) * K_PASS)
                nc.sync.dma_start(out=x_sb[t][:, half], in_=x_rows[t][:, half])
            elif name[0] == "x":
                t = int(name[1])
                nc.sync.dma_start(out=x_sb[t][:], in_=x_rows[t])
            elif name[0] == "W" and len(name) == 3:
                g = "info".index(name[1])
                c = int(name[2])
                nc.sync.dma_start(
                    out=w_raw[g][:, c], in_=w_dram[g].rearrange("(c p j) w -> c p j w", c=PASSES, j=PACK)[c]
                )
            elif name[0] == "W":
                g = "info".index(name[1])
                nc.sync.dma_start(out=w_raw[g][:], in_=w_dram[g].rearrange("(c p j) w -> p c j w", c=PASSES, j=PACK))
            elif name[0] == "U":
                g = "info".index(name[1])
                nc.sync.dma_start(out=u_sb[:, g, :], in_=u_dram[g])
            else:
                s = "hc".index(name[1])
                nc.sync.dma_start(out=pre_sb[s][:], in_=pre_layer.rearrange("s (p t) u -> s p t u", t=B_TILES)[s])

        ident_f32 = keep.tile([P, P], F32)
        make_identity(nc, ident_f32[:])
        ident_bf16 = keep.tile([P, P], BF16)
        make_identity(nc, ident_bf16[:])
        table_in = keep.tile([P, 1], F32)
        table_out = keep.tile([P, 1], F32)
        nc.vector.memset(table_in[:], 0.0)
        nc.scalar.activation(out=table_out[:], in_=table_in[:], func=ACT.Sigmoid)

        banks = {}

        def bank(name, shape, dtype):
            if name not in banks:
                banks[name] = psum.tile(shape, dtype, tag="bank", name=name)
            return banks[name]

        def unit_tile(name):
            return keep.tile([P, UNITS], F32, name=name)

        x_grouped = [keep.tile([P, PASSES * P * PACK], BF16, align_bytes=64, name="x_grouped%d" % t) for t in tiles]
        x_codes = [keep.tile([P, PASSES * P], U32, align_bytes=64, name="x_codes%d" % t) for t in tiles]
        x_scales = [keep.tile([P, PASSES * P], U8, align_bytes=64, name="x_scales%d" % t) for t in tiles]
        w_grouped = [
            keep.tile([P, PASSES, UNITS, PACK], BF16, align_bytes=64, name="w_grouped%d" % g) for g in range(GATES)
        ]
        w_codes = [keep.tile([P, PASSES * UNITS], U32, align_bytes=64, name="w_codes%d" % g) for g in range(GATES)]
        w_scales = [keep.tile([P, PASSES * UNITS], U8, align_bytes=64, name="w_scales%d" % g) for g in range(GATES)]
        hT_sb = keep.tile([P, B_TILES, P], BF16)
        rec_sb = [keep.tile([P, GATES, UNITS], F32, name="rec_sb%d" % t) for t in tiles]
        z = [[unit_tile("z%d_%d" % (g, t)) for t in tiles] for g in range(GATES)]
        gate = [[unit_tile("gate%d_%d" % (g, t)) for t in tiles] for g in range(GATES)]
        kept = [unit_tile("kept%d" % t) for t in tiles]
        fresh = [unit_tile("fresh%d" % t) for t in tiles]
        cell = [unit_tile("cell%d" % t) for t in tiles]
        cell_tanh = [unit_tile("cell_tanh%d" % t) for t in tiles]
        hidden = [unit_tile("hidden%d" % t) for t in tiles]
        out_rows = out.rearrange("s (p t) u -> s t p u", t=B_TILES)

        def xT_ps(t, c):
            return bank("xT_ps%d_%d" % (t, c), [P, PAIRS, P], F32)

        def hT_ps():
            return bank("hT_ps", [P, B_TILES, P], BF16)

        def rec_ps(t, h):
            return bank("rec_ps%d_%d" % (t, h), [P, (REC_PARTS[h].stop - REC_PARTS[h].start) * UNITS], F32)

        def acc_ps(g, t):
            return bank("acc%d_%d" % (g, t), [P, UNITS], F32)

        def transpose_x(t, c):
            x_words = x_sb[t][:].bitcast(F32).rearrange("p (c q u) -> p c u q", c=PASSES, u=PAIRS)
            for u in range(PAIRS):
                nc.tensor.transpose(xT_ps(t, c)[:, u, :], x_words[:, c, u, :], ident_f32[:])

        def regroup_x(t, c):
            grouped_words = x_grouped[t][:].bitcast(F32).rearrange("p (c b u) -> p c b u", c=PASSES, u=PAIRS)
            nc.scalar.copy(out=grouped_words[:, c], in_=xT_ps(t, c)[:].rearrange("p u b -> p b u"))

        def quantise_x(t, c):
            nc.vector.quantize_mx(
                out=x_codes[t][:, c * P : (c + 1) * P].bitcast(FP8X4),
                scales=x_scales[t][:, c * P : (c + 1) * P],
                in_=x_grouped[t][:, c * K_PASS : (c + 1) * K_PASS],
            )

        def regroup_w(g, c, copy, cols):
            copy(
                out=w_grouped[g][:, c, cols, :].rearrange("p (a i) j -> p a j i", i=RUN),
                in_=w_raw[g][:, c, :, cols].rearrange("p j (a i) -> p a j i", i=RUN),
            )

        def quantise_w(g, c):
            nc.vector.quantize_mx(
                out=w_codes[g][:, c * UNITS : (c + 1) * UNITS].bitcast(FP8X4),
                scales=w_scales[g][:, c * UNITS : (c + 1) * UNITS],
                in_=w_grouped[g][:, c].rearrange("p w j -> p (w j)"),
            )

        def transpose_h(t):
            nc.tensor.transpose(hT_ps()[:, t, :], pre_sb[0][:, t, :], ident_bf16[:])

        def copy_h():
            nc.scalar.copy(out=hT_sb[:], in_=hT_ps()[:])

        def recurrent(t, h):
            nc.tensor.matmul(
                out=rec_ps(t, h)[:],
                lhsT=hT_sb[:, t, :],
                rhs=u_sb[:, REC_PARTS[h], :].rearrange("p g u -> p (g u)"),
                start=True,
                stop=True,
            )

        def copy_recurrent(t, h):
            nc.scalar.copy(out=rec_sb[t][:, REC_PARTS[h], :].rearrange("p g u -> p (g u)"), in_=rec_ps(t, h)[:])

        def product(g, t):
            for c in range(PASSES):
                cols = slice(c * P, (c + 1) * P)
                nc.tensor.matmul_mx(
                    out=acc_ps(g, t)[:],
                    lhsT=x_codes[t][:, cols].bitcast(FP8X4),
                    lhsT_scale=x_scales[t][:, cols],
                    rhs=w_codes[g][:, cols].bitcast(FP8X4),
                    rhs_scale=w_scales[g][:, cols],
                    start=(c == 0),
                    stop=(c == PASSES - 1),
                )

        def add_gate(g, t):
            nc.vector.tensor_add(out=z[g][t][:], in0=acc_ps(g, t)[:], in1=rec_sb[t][:, g, :])

        def act_gate(g, t):
            nc.scalar.activation(out=gate[g][t][:], in_=z[g][t][:], func=gate_func[g])

        def keep_old(t):
            nc.vector.tensor_mul(out=kept[t][:], in0=gate[GATE_F][t][:], in1=pre_sb[1][:, t, :])

        def take_new(t):
            nc.vector.tensor_mul(out=fresh[t][:], in0=gate[GATE_I][t][:], in1=gate[GATE_N][t][:])

        def new_cell(t):
            nc.vector.tensor_add(out=cell[t][:], in0=kept[t][:], in1=fresh[t][:])
            nc.sync.dma_start(out=out_rows[1, t], in_=cell[t][:])

        def squash_cell(t):
            nc.scalar.activation(out=cell_tanh[t][:], in_=cell[t][:], func=ACT.Tanh)

        def new_hidden(t):
            nc.vector.tensor_mul(out=hidden[t][:], in0=gate[GATE_O][t][:], in1=cell_tanh[t][:])
            nc.sync.dma_start(out=out_rows[0, t], in_=hidden[t][:])

        def bind(f, *args):
            return lambda: f(*args)

        steps = {"hTe": copy_h}
        for t in tiles:
            s = str(t)
            steps["hT" + s] = bind(transpose_h, t)
            for h, name in enumerate("ab"):
                steps["rec" + s + name] = bind(recurrent, t, h)
                steps["rece" + s + name] = bind(copy_recurrent, t, h)
            steps["kept" + s] = bind(keep_old, t)
            steps["fresh" + s] = bind(take_new, t)
            steps["cell" + s] = bind(new_cell, t)
            steps["tc" + s] = bind(squash_cell, t)
            steps["hid" + s] = bind(new_hidden, t)
            for c in range(PASSES):
                steps["xT" + s + str(c)] = bind(transpose_x, t, c)
                steps["xe" + s + str(c)] = bind(regroup_x, t, c)
                steps["qx" + s + str(c)] = bind(quantise_x, t, c)
        for g, name in enumerate("info"):
            for c in range(PASSES):
                if VECTOR_COLS[g] > 0:
                    steps["rgV" + name + str(c)] = bind(regroup_w, g, c, nc.vector.tensor_copy, slice(0, VECTOR_COLS[g]))
                if VECTOR_COLS[g] < UNITS:
                    steps["rgS" + name + str(c)] = bind(regroup_w, g, c, nc.scalar.copy, slice(VECTOR_COLS[g], UNITS))
                steps["q" + name + str(c)] = bind(quantise_w, g, c)
            for t in tiles:
                steps["mx" + name + str(t)] = bind(product, g, t)
                steps["add" + name + str(t)] = bind(add_gate, g, t)
                steps["act" + name + str(t)] = bind(act_gate, g, t)

        for name in ORDER.split():
            steps[name]()
        assert len(ORDER.split()) == len(steps)
